import numpy as np
import ml_dtypes


def mxq(x, axis, fmt="e4m3"):
    dtype, down = {"e4m3": (ml_dtypes.float8_e4m3fn, 7), "e5m2": (ml_dtypes.float8_e5m2, 14)}[fmt]
    v = np.moveaxis(np.asarray(x, np.float32).astype(ml_dtypes.bfloat16).astype(np.float64), axis, -1)
    blocks = v.reshape(v.shape[:-1] + (-1, 32))
    amax = np.abs(blocks).max(-1, keepdims=True)
    byte = np.maximum(np.where(amax > 0, np.frexp(amax)[1] - 1 + 127, 0) - down, 1)
    scale = np.exp2(byte - 127.0)
    codes = (blocks / scale).astype(np.float32).astype(dtype).astype(np.float64)
    return np.moveaxis((codes * scale).reshape(v.shape), -1, axis)


WIDE = False


def mx_kscale(k):
    if not WIDE:
        return np.ones(k)
    levels = np.array([10, -10, 5, -5, 0])
    a = np.random.permutation(np.resize(levels, k // 512 * 4)).reshape(k // 512, 4)
    idx = np.arange(k)
    return np.exp2(a[idx // 512, idx % 128 // 32])


BF16 = ml_dtypes.bfloat16


def bf(x):
    return np.asarray(x, np.float32).astype(BF16)


def f64(x):
    return np.asarray(x).astype(np.float64)


P, N, Z, H1, H2, C = 8, 128, 16, 8192, 128, 256
EPS = 1e-5


def batch_norm(h, gamma, beta):
    mu = h.mean(axis=1, keepdims=True)
    var = h.var(axis=1, keepdims=True)
    return (h - mu) * (1.0 / np.sqrt(var + EPS)) * gamma[:, None, :] + beta[:, None, :]


def setup_inputs():
    r = np.random.standard_normal
    t = mx_kscale(H1)
    sd = np.where(np.random.random((P, 1, H1)) < 0.25, np.sqrt(EPS), 1.0)
    return {"h6_pre": bf((r((P, N, H1)) + 0.5 * r((P, 1, H1))) * sd),
            "g6": bf((1.0 + 0.1 * r((P, H1))) * t),
            "be6": bf(0.3 * r((P, H1)) * t),
            "W7": bf(r((P, H2, H1)) / np.sqrt(H1) / t),
            "b7": bf(0.3 * r((P, H2)))}


def reference(h6_pre, g6, be6, W7, b7):
    a = np.maximum(batch_norm(f64(h6_pre), f64(g6), f64(be6)), 0.0)
    y = mxq(a, 2, "e4m3") @ mxq(f64(W7), 2, "e4m3").transpose(0, 2, 1)
    return y + f64(b7)[:, None, :]

@@ -1,0 +1,209 @@
+from contextlib import ExitStack
+
+import concourse.mybir as mybir
+from concourse.masks import make_identity
+
+F32 = mybir.dt.float32
+BF16 = mybir.dt.bfloat16
+U32 = mybir.dt.uint32
+U8 = mybir.dt.uint8
+FP8X4 = mybir.dt.float8_e4m3fn_x4
+ACT = mybir.ActivationFunctionType
+ALU = mybir.AluOpType
+
+P = 128
+BLOCKS = 8
+ROWS = 128
+FEATS = 8192
+OUTS = 128
+EPS = 1e-5
+
+PACK = 4
+PAIR = 2
+GROUP_K = P * PAIR
+GROUPS = FEATS // GROUP_K
+K_PASS = P * PACK
+PASSES = FEATS // K_PASS
+BANK_GROUPS = 4
+BANK_PASSES = BANK_GROUPS * GROUP_K // K_PASS
+CHUNK_K = BANK_GROUPS * GROUP_K
+CHUNKS = FEATS // CHUNK_K
+CHUNK_COLS = BANK_PASSES * ROWS
+LOAD_K = 2048
+RUN = 4
+LAG = 2
+
+FLOPS = 2 * BLOCKS * ROWS * OUTS * FEATS
+
+
+def tile_decoder_pa_k_kernel(tc, h6_pre, g6, be6, W7, b7, out):
+    nc = tc.nc
+    with ExitStack() as ctx:
+        const = ctx.enter_context(tc.tile_pool(name="const", bufs=1))
+        h_pool = ctx.enter_context(tc.tile_pool(name="h_pool", bufs=4))
+        w_pool = ctx.enter_context(tc.tile_pool(name="w_pool", bufs=3))
+        block_pool = ctx.enter_context(tc.tile_pool(name="block_pool", bufs=2))
+        work = ctx.enter_context(tc.tile_pool(name="work", bufs=3))
+        ps_stat = ctx.enter_context(tc.psum_pool(name="ps_stat", bufs=2))
+        ps_norm = ctx.enter_context(tc.psum_pool(name="ps_norm", bufs=3))
+        ps_w = ctx.enter_context(tc.psum_pool(name="ps_w", bufs=2))
+        ps_acc = ctx.enter_context(tc.psum_pool(name="ps_acc", bufs=1))
+
+        ident = const.tile([P, P], F32)
+        make_identity(nc, ident[:])
+
+        def transpose_chunk(bank, rows_tile, c):
+            words = rows_tile[:].bitcast(F32)
+            for g in range(BANK_PASSES):
+                for u in range(PAIR):
+                    i = BANK_GROUPS * c + PAIR * g + u
+                    quarter = BANK_PASSES * u + g
+                    nc.tensor.transpose(
+                        bank[:, quarter * P : (quarter + 1) * P], words[:, i * P : (i + 1) * P], ident[:]
+                    )
+
+        affine_ps = ps_stat.tile([P, BANK_GROUPS * P], F32, tag="stat_ps")
+        for v, vec in enumerate((g6, be6)):
+            vec_rows = const.tile([P, 2, GROUP_K], BF16, name="vec_rows%d" % v)
+            nc.sync.dma_start(out=vec_rows[:], in_=vec.rearrange("(h b) (i w) -> (b i) h w", h=2, w=GROUP_K))
+            for h in range(2):
+                quarter = 2 * v + h
+                nc.tensor.transpose(
+                    affine_ps[:, quarter * P : (quarter + 1) * P], vec_rows[:, h, :].bitcast(F32), ident[:]
+                )
+        affine = const.tile([P, 2, BLOCKS, PAIR * GROUPS], F32)
+        nc.vector.tensor_copy(out=affine[:].rearrange("p v b c -> p (v b c)"), in_=affine_ps[:].bitcast(BF16))
+
+        bias_all = const.tile([P, BLOCKS * OUTS], BF16)
+        nc.scalar.dma_start(out=bias_all[:], in_=b7.rearrange("b j -> (b j)").partition_broadcast(P))
+
+        h_tiles = {}
+        w_tiles = {}
+        stats = {}
+        scales = {}
+        shifts = {}
+        a_mx = {}
+        w_mx = {}
+
+        def load(pool, src, name):
+            rows_tile = pool.tile([P, FEATS], BF16, name=name)
+            for k0 in range(0, FEATS, LOAD_K):
+                nc.sync.dma_start(out=rows_tile[:, k0 : k0 + LOAD_K], in_=src[:, k0 : k0 + LOAD_K])
+            return rows_tile
+
+        def statistics(b, c):
+            stat_ps = ps_stat.tile([P, BANK_GROUPS * P], F32)
+            transpose_chunk(stat_ps, h_tiles[b], c)
+            for g in range(BANK_PASSES):
+                for u in range(PAIR):
+                    i = BANK_GROUPS * c + PAIR * g + u
+                    quarter = BANK_PASSES * u + g
+                    nc.vector.bn_stats(
+                        out=stats[b][:, i, :], in_=stat_ps[:, quarter * P : (quarter + 1) * P].bitcast(BF16)
+                    )
+
+        def scale_and_shift(b):
+            moments = stats[b][:].rearrange("p i (e s) -> p s (i e)", s=3)
+            var_eps = work.tile([P, PAIR * GROUPS], F32)
+            nc.vector.tensor_scalar(
+                out=var_eps[:], in0=moments[:, 2, :], scalar1=1.0 / ROWS, scalar2=EPS, op0=ALU.mult, op1=ALU.add
+            )
+            std = work.tile([P, PAIR * GROUPS], F32)
+            nc.scalar.sqrt(out=std[:], in_=var_eps[:])
+            rstd = work.tile([P, PAIR * GROUPS], F32)
+            nc.vector.reciprocal(out=rstd[:], in_=std[:])
+            scale = block_pool.tile([P, PAIR * GROUPS], F32)
+            nc.vector.tensor_mul(out=scale[:], in0=rstd[:], in1=affine[:, 0, b, :])
+            mean_scaled = work.tile([P, PAIR * GROUPS], F32)
+            nc.vector.tensor_mul(out=mean_scaled[:], in0=moments[:, 1, :], in1=scale[:])
+            shift = block_pool.tile([P, PAIR * GROUPS], F32)
+            nc.vector.tensor_sub(out=shift[:], in0=affine[:, 1, b, :], in1=mean_scaled[:])
+            scales[b] = scale
+            shifts[b] = shift
+
+        def quantise(grouped, mx, c):
+            codes, planes = mx
+            cols = slice(c * CHUNK_COLS, (c + 1) * CHUNK_COLS)
+            nc.vector.quantize_mx(
+                out=codes[:, cols].bitcast(FP8X4),
+                scales=planes[:, cols],
+                in_=grouped[:].rearrange("p m t -> p (m t)"),
+            )
+
+        def weights(b, c):
+            w_ps = ps_w.tile([P, BANK_GROUPS * P], F32)
+            transpose_chunk(w_ps, w_tiles[b], c)
+            w_grouped = work.tile([P, CHUNK_COLS, PACK], BF16, align_bytes=64)
+            nc.scalar.copy(
+                out=w_grouped[:].rearrange("p m t -> p (m t)").bitcast(F32).rearrange("p (m u) -> p m u", u=PAIR),
+                in_=w_ps[:].rearrange("p (u m) -> p m u", u=PAIR),
+            )
+            quantise(w_grouped, w_mx[b], c)
+
+        def activations(b, c):
+            norm_ps = ps_norm.tile([P, BANK_GROUPS * P], F32)
+            transpose_chunk(norm_ps, h_tiles[b], c)
+            halves = norm_ps[:].bitcast(BF16).rearrange("p (u g n e) -> p u g n e", u=PAIR, g=BANK_PASSES, e=PAIR)
+            a_planes = work.tile([P, PACK, CHUNK_COLS], BF16)
+            for g in range(BANK_PASSES):
+                for u in range(PAIR):
+                    for e in range(PAIR):
+                        col = PAIR * (BANK_GROUPS * c + PAIR * g + u) + e
+                        nc.scalar.activation(
+                            out=a_planes[:, PAIR * u + e, g * ROWS : (g + 1) * ROWS],
+                            in_=halves[:, u, g, :, e],
+                            func=ACT.Relu,
+                            scale=scales[b][:, col : col + 1],
+                            bias=shifts[b][:, col : col + 1],
+                        )
+            a_grouped = work.tile([P, CHUNK_COLS, PACK], BF16, align_bytes=64)
+            nc.vector.tensor_copy(
+                out=a_grouped[:].rearrange("p (c i) t -> p c t i", i=RUN),
+                in_=a_planes[:].rearrange("p t (c i) -> p c t i", i=RUN),
+            )
+            quantise(a_grouped, a_mx[b], c)
+
+        def multiply(b):
+            a_codes, a_planes = a_mx[b]
+            w_codes, w_planes = w_mx[b]
+            acc = ps_acc.tile([P, OUTS], F32)
+            for s in range(PASSES):
+                cols = slice(s * P, (s + 1) * P)
+                nc.tensor.matmul_mx(
+                    out=acc[:],
+                    lhsT=a_codes[:, cols].bitcast(FP8X4),
+                    lhsT_scale=a_planes[:, cols],
+                    rhs=w_codes[:, cols].bitcast(FP8X4),
+                    rhs_scale=w_planes[:, cols],
+                    start=(s == 0),
+                    stop=(s == PASSES - 1),
+                )
+            result = work.tile([P, OUTS], F32)
+            nc.vector.tensor_add(out=result[:], in0=acc[:], in1=bias_all[:, b * OUTS : (b + 1) * OUTS])
+            nc.sync.dma_start(out=out[b], in_=result[:])
+
+        def mx_tiles(name):
+            codes = block_pool.tile([P, PASSES * P], U32, name=name + "_codes", align_bytes=64)
+            planes = block_pool.tile([P, PASSES * P], U8, name=name + "_scales", align_bytes=64)
+            return codes, planes
+
+        for step in range(BLOCKS * CHUNKS + CHUNKS + LAG):
+            if step < BLOCKS * CHUNKS:
+                b, c = divmod(step, CHUNKS)
+                if c == 0:
+                    h_tiles[b] = load(h_pool, h6_pre[b], "h_rows")
+                    w_tiles[b] = load(w_pool, W7[b], "w_rows")
+                    block_stats = block_pool.tile([P, GROUPS, 6], F32)
+                    stats[b] = block_stats
+                statistics(b, c)
+                if c == CHUNKS - 1:
+                    scale_and_shift(b)
+            if step >= CHUNKS + LAG:
+                b, c = divmod(step - CHUNKS - LAG, CHUNKS)
+                if c == 0:
+                    a_mx[b] = mx_tiles("a")
+                    w_mx[b] = mx_tiles("w")
+                weights(b, c)
+                activations(b, c)
+                if c == CHUNKS - 1:
+                    multiply(b)

@@ -21,17 +21,21 @@ EPS = 1e-5
 PACK = 4
 PAIR = 2
 GROUP_K = P * PAIR
-GROUPS = FEATS // GROUP_K
 K_PASS = P * PACK
 PASSES = FEATS // K_PASS
 BANK_GROUPS = 4
-BANK_PASSES = BANK_GROUPS * GROUP_K // K_PASS
-CHUNK_K = BANK_GROUPS * GROUP_K
-CHUNKS = FEATS // CHUNK_K
-CHUNK_COLS = BANK_PASSES * ROWS
-LOAD_K = 2048
-RUN = 4
-LAG = 2
+BANK_PASSES = 2
+BANK_COLS = BANK_PASSES * ROWS
+BATCH_BANKS = 2
+BATCH_K = BATCH_BANKS * BANK_GROUPS * GROUP_K
+BATCH_GROUPS = BATCH_BANKS * BANK_GROUPS
+BATCH_FEATS = BATCH_GROUPS * PAIR
+BATCH_PASSES = BATCH_BANKS * BANK_PASSES
+BATCH_COLS = BATCH_BANKS * BANK_COLS
+BLOCK_BATCHES = FEATS // BATCH_K
+BATCHES = BLOCKS * BLOCK_BATCHES
+A_LAG = 3
+PREFETCH = 6
 
 FLOPS = 2 * BLOCKS * ROWS * OUTS * FEATS
 
@@ -40,29 +44,31 @@ def tile_decoder_pa_k_kernel(tc, h6_pre, g6, be6, W7, b7, out):
     nc = tc.nc
     with ExitStack() as ctx:
         const = ctx.enter_context(tc.tile_pool(name="const", bufs=1))
-        h_pool = ctx.enter_context(tc.tile_pool(name="h_pool", bufs=4))
-        w_pool = ctx.enter_context(tc.tile_pool(name="w_pool", bufs=3))
+        rows_pool = ctx.enter_context(tc.tile_pool(name="rows_pool", bufs=PREFETCH + 2))
         block_pool = ctx.enter_context(tc.tile_pool(name="block_pool", bufs=2))
         work = ctx.enter_context(tc.tile_pool(name="work", bufs=3))
-        ps_stat = ctx.enter_context(tc.psum_pool(name="ps_stat", bufs=2))
-        ps_norm = ctx.enter_context(tc.psum_pool(name="ps_norm", bufs=3))
-        ps_w = ctx.enter_context(tc.psum_pool(name="ps_w", bufs=2))
+        ps_h = ctx.enter_context(tc.psum_pool(name="ps_h", bufs=3 * BATCH_BANKS))
+        ps_w = ctx.enter_context(tc.psum_pool(name="ps_w", bufs=1))
         ps_acc = ctx.enter_context(tc.psum_pool(name="ps_acc", bufs=1))
 
         ident = const.tile([P, P], F32)
         make_identity(nc, ident[:])
+        zero_col = const.tile([P, 1], F32)
+        nc.vector.memset(zero_col[:], 0.0)
+        eps_col = const.tile([P, 1], F32)
+        nc.vector.tensor_scalar(out=eps_col[:], in0=zero_col[:], scalar1=1.0, scalar2=EPS, op0=ALU.mult, op1=ALU.add)
 
-        def transpose_chunk(bank, rows_tile, c):
+        def transpose_bank(bank, rows_tile, ci):
             words = rows_tile[:].bitcast(F32)
             for g in range(BANK_PASSES):
                 for u in range(PAIR):
-                    i = BANK_GROUPS * c + PAIR * g + u
+                    i = BANK_GROUPS * ci + PAIR * g + u
                     quarter = BANK_PASSES * u + g
                     nc.tensor.transpose(
                         bank[:, quarter * P : (quarter + 1) * P], words[:, i * P : (i + 1) * P], ident[:]
                     )
 
-        affine_ps = ps_stat.tile([P, BANK_GROUPS * P], F32, tag="stat_ps")
+        affine_ps = ps_h.tile([P, BANK_GROUPS * P], F32, tag="h_ps")
         for v, vec in enumerate((g6, be6)):
             vec_rows = const.tile([P, 2, GROUP_K], BF16, name="vec_rows%d" % v)
             nc.sync.dma_start(out=vec_rows[:], in_=vec.rearrange("(h b) (i w) -> (b i) h w", h=2, w=GROUP_K))
@@ -71,139 +77,219 @@ def tile_decoder_pa_k_kernel(tc, h6_pre, g6, be6, W7, b7, out):
                 nc.tensor.transpose(
                     affine_ps[:, quarter * P : (quarter + 1) * P], vec_rows[:, h, :].bitcast(F32), ident[:]
                 )
-        affine = const.tile([P, 2, BLOCKS, PAIR * GROUPS], F32)
-        nc.vector.tensor_copy(out=affine[:].rearrange("p v b c -> p (v b c)"), in_=affine_ps[:].bitcast(BF16))
+        affine = const.tile([P, 2, BATCHES * BATCH_FEATS], F32)
+        nc.vector.tensor_copy(out=affine[:].rearrange("p v c -> p (v c)"), in_=affine_ps[:].bitcast(BF16))
 
         bias_all = const.tile([P, BLOCKS * OUTS], BF16)
         nc.scalar.dma_start(out=bias_all[:], in_=b7.rearrange("b j -> (b j)").partition_broadcast(P))
 
-        h_tiles = {}
-        w_tiles = {}
+        h_rows = {}
+        w_rows = {}
+        h_banks = {}
+        w_banks = {}
         stats = {}
+        stds = {}
+        gain_means = {}
+        rstds = {}
+        means_scaled = {}
         scales = {}
         shifts = {}
+        a_planes = {}
+        a_grouped = {}
+        w_grouped = {}
         a_mx = {}
         w_mx = {}
+        accs = {}
 
-        def load(pool, src, name):
-            rows_tile = pool.tile([P, FEATS], BF16, name=name)
-            for k0 in range(0, FEATS, LOAD_K):
-                nc.sync.dma_start(out=rows_tile[:, k0 : k0 + LOAD_K], in_=src[:, k0 : k0 + LOAD_K])
-            return rows_tile
+        def batch_feats(t):
+            return slice(t * BATCH_FEATS, (t + 1) * BATCH_FEATS)
 
-        def statistics(b, c):
-            stat_ps = ps_stat.tile([P, BANK_GROUPS * P], F32)
-            transpose_chunk(stat_ps, h_tiles[b], c)
-            for g in range(BANK_PASSES):
-                for u in range(PAIR):
-                    i = BANK_GROUPS * c + PAIR * g + u
-                    quarter = BANK_PASSES * u + g
-                    nc.vector.bn_stats(
-                        out=stats[b][:, i, :], in_=stat_ps[:, quarter * P : (quarter + 1) * P].bitcast(BF16)
+        def load(t):
+            b, r = divmod(t, BLOCK_BATCHES)
+            feats = slice(r * BATCH_K, (r + 1) * BATCH_K)
+            h_tile = rows_pool.tile([P, BATCH_K], BF16)
+            nc.sync.dma_start(out=h_tile[:], in_=h6_pre[b][:, feats])
+            w_tile = rows_pool.tile([P, BATCH_K], BF16)
+            nc.sync.dma_start(out=w_tile[:], in_=W7[b][:, feats])
+            h_rows[t] = h_tile
+            w_rows[t] = w_tile
+
+        def transpose_h(t, ci):
+            h_ps = ps_h.tile([P, BANK_GROUPS * P], F32)
+            transpose_bank(h_ps, h_rows[t], ci)
+            h_banks[t, ci] = h_ps
+
+        def statistics(t):
+            batch_stats = work.tile([P, BATCH_GROUPS, 6], F32)
+            for ci in range(BATCH_BANKS):
+                for g in range(BANK_PASSES):
+                    for u in range(PAIR):
+                        quarter = BANK_PASSES * u + g
+                        nc.vector.bn_stats(
+                            out=batch_stats[:, BANK_GROUPS * ci + PAIR * g + u, :],
+                            in_=h_banks[t, ci][:, quarter * P : (quarter + 1) * P].bitcast(BF16),
+                        )
+            stats[t] = batch_stats[:].rearrange("p i (e s) -> p s (i e)", s=3)
+
+        def spread(t):
+            std = work.tile([P, BATCH_FEATS], F32)
+            nc.scalar.activation(out=std[:], in_=stats[t][:, 2, :], func=ACT.Sqrt, scale=1.0 / ROWS, bias=eps_col[:])
+            stds[t] = std
+
+        def gain_times_mean(t):
+            gain_mean = work.tile([P, BATCH_FEATS], F32)
+            nc.vector.tensor_mul(out=gain_mean[:], in0=stats[t][:, 1, :], in1=affine[:, 0, batch_feats(t)])
+            gain_means[t] = gain_mean
+
+        def inverse_spread(t):
+            rstd = work.tile([P, BATCH_FEATS], F32)
+            nc.vector.reciprocal(out=rstd[:], in_=stds[t][:])
+            rstds[t] = rstd
+
+        def scale_terms(t):
+            scale = work.tile([P, BATCH_FEATS], F32)
+            nc.vector.tensor_mul(out=scale[:], in0=rstds[t][:], in1=affine[:, 0, batch_feats(t)])
+            mean_scaled = work.tile([P, BATCH_FEATS], F32)
+            nc.vector.tensor_mul(out=mean_scaled[:], in0=rstds[t][:], in1=gain_means[t][:])
+            scales[t] = scale
+            means_scaled[t] = mean_scaled
+
+        def shift_term(t):
+            shift = work.tile([P, BATCH_FEATS], F32)
+            nc.vector.tensor_sub(out=shift[:], in0=affine[:, 1, batch_feats(t)], in1=means_scaled[t][:])
+            shifts[t] = shift
+
+        def activations(t, ci, g):
+            if ci == 0 and g == 0:
+                planes_tile = work.tile([P, PACK, BATCH_COLS], BF16)
+                a_planes[t] = planes_tile
+            halves = h_banks[t, ci][:].bitcast(BF16).rearrange(
+                "p (u g n e) -> p u g n e", u=PAIR, g=BANK_PASSES, e=PAIR
+            )
+            first = ci * BANK_COLS + g * ROWS
+            for u in range(PAIR):
+                for e in range(PAIR):
+                    col = PAIR * (BANK_GROUPS * ci + PAIR * g + u) + e
+                    nc.scalar.activation(
+                        out=a_planes[t][:, PAIR * u + e, first : first + ROWS],
+                        in_=halves[:, u, g, :, e],
+                        func=ACT.Relu,
+                        scale=scales[t][:, col : col + 1],
+                        bias=shifts[t][:, col : col + 1],
                     )
 
-        def scale_and_shift(b):
-            moments = stats[b][:].rearrange("p i (e s) -> p s (i e)", s=3)
-            var_eps = work.tile([P, PAIR * GROUPS], F32)
-            nc.vector.tensor_scalar(
-                out=var_eps[:], in0=moments[:, 2, :], scalar1=1.0 / ROWS, scalar2=EPS, op0=ALU.mult, op1=ALU.add
+        def regroup(t):
+            grouped_tile = work.tile([P, BATCH_COLS, PACK], BF16, name="a_grouped", align_bytes=64)
+            nc.gpsimd.tensor_scalar(
+                out=grouped_tile[:],
+                in0=a_planes[t][:].rearrange("p t m -> p m t"),
+                scalar1=1.0,
+                scalar2=0.0,
+                op0=ALU.mult,
+                op1=ALU.add,
             )
-            std = work.tile([P, PAIR * GROUPS], F32)
-            nc.scalar.sqrt(out=std[:], in_=var_eps[:])
-            rstd = work.tile([P, PAIR * GROUPS], F32)
-            nc.vector.reciprocal(out=rstd[:], in_=std[:])
-            scale = block_pool.tile([P, PAIR * GROUPS], F32)
-            nc.vector.tensor_mul(out=scale[:], in0=rstd[:], in1=affine[:, 0, b, :])
-            mean_scaled = work.tile([P, PAIR * GROUPS], F32)
-            nc.vector.tensor_mul(out=mean_scaled[:], in0=moments[:, 1, :], in1=scale[:])
-            shift = block_pool.tile([P, PAIR * GROUPS], F32)
-            nc.vector.tensor_sub(out=shift[:], in0=affine[:, 1, b, :], in1=mean_scaled[:])
-            scales[b] = scale
-            shifts[b] = shift
+            a_grouped[t] = grouped_tile
 
-        def quantise(grouped, mx, c):
-            codes, planes = mx
-            cols = slice(c * CHUNK_COLS, (c + 1) * CHUNK_COLS)
-            nc.vector.quantize_mx(
-                out=codes[:, cols].bitcast(FP8X4),
-                scales=planes[:, cols],
-                in_=grouped[:].rearrange("p m t -> p (m t)"),
-            )
-
-        def weights(b, c):
+        def transpose_w(t, ci):
             w_ps = ps_w.tile([P, BANK_GROUPS * P], F32)
-            transpose_chunk(w_ps, w_tiles[b], c)
-            w_grouped = work.tile([P, CHUNK_COLS, PACK], BF16, align_bytes=64)
+            transpose_bank(w_ps, w_rows[t], ci)
+            w_banks[t, ci] = w_ps
+
+        def copy_w(t, ci):
+            if ci == 0:
+                grouped_tile = work.tile([P, BATCH_COLS, PACK], BF16, name="w_grouped", align_bytes=64)
+                w_grouped[t] = grouped_tile
+            part = w_grouped[t][:, ci * BANK_COLS : (ci + 1) * BANK_COLS, :]
             nc.scalar.copy(
-                out=w_grouped[:].rearrange("p m t -> p (m t)").bitcast(F32).rearrange("p (m u) -> p m u", u=PAIR),
-                in_=w_ps[:].rearrange("p (u m) -> p m u", u=PAIR),
+                out=part.rearrange("p m t -> p (m t)").bitcast(F32).rearrange("p (m u) -> p m u", u=PAIR),
+                in_=w_banks[t, ci][:].rearrange("p (u m) -> p m u", u=PAIR),
             )
-            quantise(w_grouped, w_mx[b], c)
 
-        def activations(b, c):
-            norm_ps = ps_norm.tile([P, BANK_GROUPS * P], F32)
-            transpose_chunk(norm_ps, h_tiles[b], c)
-            halves = norm_ps[:].bitcast(BF16).rearrange("p (u g n e) -> p u g n e", u=PAIR, g=BANK_PASSES, e=PAIR)
-            a_planes = work.tile([P, PACK, CHUNK_COLS], BF16)
-            for g in range(BANK_PASSES):
-                for u in range(PAIR):
-                    for e in range(PAIR):
-                        col = PAIR * (BANK_GROUPS * c + PAIR * g + u) + e
-                        nc.scalar.activation(
-                            out=a_planes[:, PAIR * u + e, g * ROWS : (g + 1) * ROWS],
-                            in_=halves[:, u, g, :, e],
-                            func=ACT.Relu,
-                            scale=scales[b][:, col : col + 1],
-                            bias=shifts[b][:, col : col + 1],
-                        )
-            a_grouped = work.tile([P, CHUNK_COLS, PACK], BF16, align_bytes=64)
-            nc.vector.tensor_copy(
-                out=a_grouped[:].rearrange("p (c i) t -> p c t i", i=RUN),
-                in_=a_planes[:].rearrange("p t (c i) -> p c t i", i=RUN),
+        def quantise(grouped, mx, name, t, ci):
+            b, r = divmod(t, BLOCK_BATCHES)
+            if r == 0 and ci == 0:
+                codes_tile = block_pool.tile([P, PASSES * P], U32, name=name + "_codes", align_bytes=64)
+                scale_bytes = block_pool.tile([P, PASSES * P], U8, name=name + "_scale_bytes", align_bytes=64)
+                mx[b] = (codes_tile, scale_bytes)
+            codes_tile, scale_bytes = mx[b]
+            first = r * BATCH_COLS + ci * BANK_COLS
+            cols = slice(first, first + BANK_COLS)
+            nc.vector.quantize_mx(
+                out=codes_tile[:, cols].bitcast(FP8X4),
+                scales=scale_bytes[:, cols],
+                in_=grouped[t][:, ci * BANK_COLS : (ci + 1) * BANK_COLS, :].rearrange("p m t -> p (m t)"),
             )
-            quantise(a_grouped, a_mx[b], c)
 
-        def multiply(b):
-            a_codes, a_planes = a_mx[b]
-            w_codes, w_planes = w_mx[b]
-            acc = ps_acc.tile([P, OUTS], F32)
-            for s in range(PASSES):
+        def multiply(t):
+            b, r = divmod(t, BLOCK_BATCHES)
+            a_codes, a_scale_bytes = a_mx[b]
+            w_codes, w_scale_bytes = w_mx[b]
+            if r == 0:
+                acc = ps_acc.tile([P, OUTS], F32)
+                accs[b] = acc
+            for s in range(r * BATCH_PASSES, (r + 1) * BATCH_PASSES):
                 cols = slice(s * P, (s + 1) * P)
                 nc.tensor.matmul_mx(
-                    out=acc[:],
+                    out=accs[b][:],
                     lhsT=a_codes[:, cols].bitcast(FP8X4),
-                    lhsT_scale=a_planes[:, cols],
+                    lhsT_scale=a_scale_bytes[:, cols],
                     rhs=w_codes[:, cols].bitcast(FP8X4),
-                    rhs_scale=w_planes[:, cols],
+                    rhs_scale=w_scale_bytes[:, cols],
                     start=(s == 0),
                     stop=(s == PASSES - 1),
                 )
+
+        def finish(b):
             result = work.tile([P, OUTS], F32)
-            nc.vector.tensor_add(out=result[:], in0=acc[:], in1=bias_all[:, b * OUTS : (b + 1) * OUTS])
+            nc.vector.tensor_add(out=result[:], in0=accs[b][:], in1=bias_all[:, b * OUTS : (b + 1) * OUTS])
             nc.sync.dma_start(out=out[b], in_=result[:])
 
-        def mx_tiles(name):
-            codes = block_pool.tile([P, PASSES * P], U32, name=name + "_codes", align_bytes=64)
-            planes = block_pool.tile([P, PASSES * P], U8, name=name + "_scales", align_bytes=64)
-            return codes, planes
+        def live(t):
+            return 0 <= t < BATCHES
 
-        for step in range(BLOCKS * CHUNKS + CHUNKS + LAG):
-            if step < BLOCKS * CHUNKS:
-                b, c = divmod(step, CHUNKS)
-                if c == 0:
-                    h_tiles[b] = load(h_pool, h6_pre[b], "h_rows")
-                    w_tiles[b] = load(w_pool, W7[b], "w_rows")
-                    block_stats = block_pool.tile([P, GROUPS, 6], F32)
-                    stats[b] = block_stats
-                statistics(b, c)
-                if c == CHUNKS - 1:
-                    scale_and_shift(b)
-            if step >= CHUNKS + LAG:
-                b, c = divmod(step - CHUNKS - LAG, CHUNKS)
-                if c == 0:
-                    a_mx[b] = mx_tiles("a")
-                    w_mx[b] = mx_tiles("w")
-                weights(b, c)
-                activations(b, c)
-                if c == CHUNKS - 1:
-                    multiply(b)
+        with tc.manual_schedule():
+            for t in range(PREFETCH):
+                load(t)
+            for ci in range(BATCH_BANKS):
+                transpose_h(0, ci)
+            transpose_w(0, 0)
+            for t in range(BATCHES + A_LAG + 1):
+                if live(t + PREFETCH):
+                    load(t + PREFETCH)
+                if live(t - A_LAG - 1):
+                    multiply(t - A_LAG - 1)
+                if live(t):
+                    statistics(t)
+                for ci in range(BATCH_BANKS):
+                    if live(t + 1):
+                        transpose_h(t + 1, ci)
+                    for g in range(BANK_PASSES):
+                        if live(t - 1):
+                            activations(t - 1, ci, g)
+                        if live(t) and ci == BATCH_BANKS - 1 and g == 0:
+                            spread(t)
+                    if live(t):
+                        copy_w(t, ci)
+                    t_next, ci_next = divmod(t * BATCH_BANKS + ci + 1, BATCH_BANKS)
+                    if live(t) and live(t_next):
+                        transpose_w(t_next, ci_next)
+                if live(t - 1):
+                    regroup(t - 1)
+                if live(t - A_LAG):
+                    quantise(a_grouped, a_mx, "a", t - A_LAG, 0)
+                if live(t):
+                    gain_times_mean(t)
+                if live(t - A_LAG):
+                    quantise(a_grouped, a_mx, "a", t - A_LAG, 1)
+                if live(t):
+                    inverse_spread(t)
+                if live(t - 1):
+                    quantise(w_grouped, w_mx, "w", t - 1, 0)
+                if live(t):
+                    scale_terms(t)
+                if live(t - 1):
+                    quantise(w_grouped, w_mx, "w", t - 1, 1)
+                if live(t):
+                    shift_term(t)
+                if live(t - A_LAG - 1) and (t - A_LAG - 1) % BLOCK_BATCHES == BLOCK_BATCHES - 1:
+                    finish((t - A_LAG - 1) // BLOCK_BATCHES)

@@ -34,6 +34,7 @@ BATCH_PASSES = BATCH_BANKS * BANK_PASSES
 BATCH_COLS = BATCH_BANKS * BANK_COLS
 BLOCK_BATCHES = FEATS // BATCH_K
 BATCHES = BLOCKS * BLOCK_BATCHES
+RUN = 4
 A_LAG = 3
 PREFETCH = 6
 
@@ -181,8 +182,8 @@ def tile_decoder_pa_k_kernel(tc, h6_pre, g6, be6, W7, b7, out):
         def regroup(t):
             grouped_tile = work.tile([P, BATCH_COLS, PACK], BF16, name="a_grouped", align_bytes=64)
             nc.gpsimd.tensor_scalar(
-                out=grouped_tile[:],
-                in0=a_planes[t][:].rearrange("p t m -> p m t"),
+                out=grouped_tile[:].rearrange("p (c i) t -> p c t i", i=RUN),
+                in0=a_planes[t][:].rearrange("p t (c i) -> p c t i", i=RUN),
                 scalar1=1.0,
                 scalar2=0.0,
                 op0=ALU.mult,

@@ -72,7 +72,7 @@ def tile_decoder_pa_k_kernel(tc, h6_pre, g6, be6, W7, b7, out):
         affine_ps = ps_h.tile([P, BANK_GROUPS * P], F32, tag="h_ps")
         for v, vec in enumerate((g6, be6)):
             vec_rows = const.tile([P, 2, GROUP_K], BF16, name="vec_rows%d" % v)
-            nc.sync.dma_start(out=vec_rows[:], in_=vec.rearrange("(h b) (i w) -> (b i) h w", h=2, w=GROUP_K))
+            nc.scalar.dma_start(out=vec_rows[:], in_=vec.rearrange("(h b) (i w) -> (b i) h w", h=2, w=GROUP_K))
             for h in range(2):
                 quarter = 2 * v + h
                 nc.tensor.transpose(
@@ -82,7 +82,6 @@ def tile_decoder_pa_k_kernel(tc, h6_pre, g6, be6, W7, b7, out):
         nc.vector.tensor_copy(out=affine[:].rearrange("p v c -> p (v c)"), in_=affine_ps[:].bitcast(BF16))
 
         bias_all = const.tile([P, BLOCKS * OUTS], BF16)
-        nc.scalar.dma_start(out=bias_all[:], in_=b7.rearrange("b j -> (b j)").partition_broadcast(P))
 
         h_rows = {}
         w_rows = {}
@@ -251,6 +250,7 @@ def tile_decoder_pa_k_kernel(tc, h6_pre, g6, be6, W7, b7, out):
         with tc.manual_schedule():
             for t in range(PREFETCH):
                 load(t)
+            nc.sync.dma_start(out=bias_all[:], in_=b7.rearrange("b j -> (b j)").partition_broadcast(P))
             for ci in range(BATCH_BANKS):
                 transpose_h(0, ci)
             transpose_w(0, 0)

from contextlib import ExitStack

import concourse.mybir as mybir
from concourse.masks import make_identity

F32 = mybir.dt.float32
BF16 = mybir.dt.bfloat16
U32 = mybir.dt.uint32
U8 = mybir.dt.uint8
FP8X4 = mybir.dt.float8_e4m3fn_x4
ACT = mybir.ActivationFunctionType
ALU = mybir.AluOpType

P = 128
BLOCKS = 8
ROWS = 128
FEATS = 8192
OUTS = 128
EPS = 1e-5

PACK = 4
PAIR = 2
GROUP_K = P * PAIR
K_PASS = P * PACK
PASSES = FEATS // K_PASS
BANK_GROUPS = 4
BANK_PASSES = 2
BANK_COLS = BANK_PASSES * ROWS
BATCH_BANKS = 2
BATCH_K = BATCH_BANKS * BANK_GROUPS * GROUP_K
BATCH_GROUPS = BATCH_BANKS * BANK_GROUPS
BATCH_FEATS = BATCH_GROUPS * PAIR
BATCH_PASSES = BATCH_BANKS * BANK_PASSES
BATCH_COLS = BATCH_BANKS * BANK_COLS
BLOCK_BATCHES = FEATS // BATCH_K
BATCHES = BLOCKS * BLOCK_BATCHES
RUN = 4
A_LAG = 3
PREFETCH = 6

FLOPS = 2 * BLOCKS * ROWS * OUTS * FEATS


def tile_decoder_pa_k_kernel(tc, h6_pre, g6, be6, W7, b7, out):
    nc = tc.nc
    with ExitStack() as ctx:
        const = ctx.enter_context(tc.tile_pool(name="const", bufs=1))
        rows_pool = ctx.enter_context(tc.tile_pool(name="rows_pool", bufs=PREFETCH + 2))
        block_pool = ctx.enter_context(tc.tile_pool(name="block_pool", bufs=2))
        work = ctx.enter_context(tc.tile_pool(name="work", bufs=3))
        ps_h = ctx.enter_context(tc.psum_pool(name="ps_h", bufs=3 * BATCH_BANKS))
        ps_w = ctx.enter_context(tc.psum_pool(name="ps_w", bufs=1))
        ps_acc = ctx.enter_context(tc.psum_pool(name="ps_acc", bufs=1))

        ident = const.tile([P, P], F32)
        make_identity(nc, ident[:])
        zero_col = const.tile([P, 1], F32)
        nc.vector.memset(zero_col[:], 0.0)
        eps_col = const.tile([P, 1], F32)
        nc.vector.tensor_scalar(out=eps_col[:], in0=zero_col[:], scalar1=1.0, scalar2=EPS, op0=ALU.mult, op1=ALU.add)

        def transpose_bank(bank, rows_tile, ci):
            words = rows_tile[:].bitcast(F32)
            for g in range(BANK_PASSES):
                for u in range(PAIR):
                    i = BANK_GROUPS * ci + PAIR * g + u
                    quarter = BANK_PASSES * u + g
                    nc.tensor.transpose(
                        bank[:, quarter * P : (quarter + 1) * P], words[:, i * P : (i + 1) * P], ident[:]
                    )

        affine_ps = ps_h.tile([P, BANK_GROUPS * P], F32, tag="h_ps")
        for v, vec in enumerate((g6, be6)):
            vec_rows = const.tile([P, 2, GROUP_K], BF16, name="vec_rows%d" % v)
            nc.scalar.dma_start(out=vec_rows[:], in_=vec.rearrange("(h b) (i w) -> (b i) h w", h=2, w=GROUP_K))
            for h in range(2):
                quarter = 2 * v + h
                nc.tensor.transpose(
                    affine_ps[:, quarter * P : (quarter + 1) * P], vec_rows[:, h, :].bitcast(F32), ident[:]
                )
        affine = const.tile([P, 2, BATCHES * BATCH_FEATS], F32)
        nc.vector.tensor_copy(out=affine[:].rearrange("p v c -> p (v c)"), in_=affine_ps[:].bitcast(BF16))

        bias_all = const.tile([P, BLOCKS * OUTS], BF16)

        h_rows = {}
        w_rows = {}
        h_banks = {}
        w_banks = {}
        stats = {}
        stds = {}
        gain_means = {}
        rstds = {}
        means_scaled = {}
        scales = {}
        shifts = {}
        a_planes = {}
        a_grouped = {}
        w_grouped = {}
        a_mx = {}
        w_mx = {}
        accs = {}

        def batch_feats(t):
            return slice(t * BATCH_FEATS, (t + 1) * BATCH_FEATS)

        def load(t):
            b, r = divmod(t, BLOCK_BATCHES)
            feats = slice(r * BATCH_K, (r + 1) * BATCH_K)
            h_tile = rows_pool.tile([P, BATCH_K], BF16)
            nc.sync.dma_start(out=h_tile[:], in_=h6_pre[b][:, feats])
            w_tile = rows_pool.tile([P, BATCH_K], BF16)
            nc.sync.dma_start(out=w_tile[:], in_=W7[b][:, feats])
            h_rows[t] = h_tile
            w_rows[t] = w_tile

        def transpose_h(t, ci):
            h_ps = ps_h.tile([P, BANK_GROUPS * P], F32)
            transpose_bank(h_ps, h_rows[t], ci)
            h_banks[t, ci] = h_ps

        def statistics(t):
            batch_stats = work.tile([P, BATCH_GROUPS, 6], F32)
            for ci in range(BATCH_BANKS):
                for g in range(BANK_PASSES):
                    for u in range(PAIR):
                        quarter = BANK_PASSES * u + g
                        nc.vector.bn_stats(
                            out=batch_stats[:, BANK_GROUPS * ci + PAIR * g + u, :],
                            in_=h_banks[t, ci][:, quarter * P : (quarter + 1) * P].bitcast(BF16),
                        )
            stats[t] = batch_stats[:].rearrange("p i (e s) -> p s (i e)", s=3)

        def spread(t):
            std = work.tile([P, BATCH_FEATS], F32)
            nc.scalar.activation(out=std[:], in_=stats[t][:, 2, :], func=ACT.Sqrt, scale=1.0 / ROWS, bias=eps_col[:])
            stds[t] = std

        def gain_times_mean(t):
            gain_mean = work.tile([P, BATCH_FEATS], F32)
            nc.vector.tensor_mul(out=gain_mean[:], in0=stats[t][:, 1, :], in1=affine[:, 0, batch_feats(t)])
            gain_means[t] = gain_mean

        def inverse_spread(t):
            rstd = work.tile([P, BATCH_FEATS], F32)
            nc.vector.reciprocal(out=rstd[:], in_=stds[t][:])
            rstds[t] = rstd

        def scale_terms(t):
            scale = work.tile([P, BATCH_FEATS], F32)
            nc.vector.tensor_mul(out=scale[:], in0=rstds[t][:], in1=affine[:, 0, batch_feats(t)])
            mean_scaled = work.tile([P, BATCH_FEATS], F32)
            nc.vector.tensor_mul(out=mean_scaled[:], in0=rstds[t][:], in1=gain_means[t][:])
            scales[t] = scale
            means_scaled[t] = mean_scaled

        def shift_term(t):
            shift = work.tile([P, BATCH_FEATS], F32)
            nc.vector.tensor_sub(out=shift[:], in0=affine[:, 1, batch_feats(t)], in1=means_scaled[t][:])
            shifts[t] = shift

        def activations(t, ci, g):
            if ci == 0 and g == 0:
                planes_tile = work.tile([P, PACK, BATCH_COLS], BF16)
                a_planes[t] = planes_tile
            halves = h_banks[t, ci][:].bitcast(BF16).rearrange(
                "p (u g n e) -> p u g n e", u=PAIR, g=BANK_PASSES, e=PAIR
            )
            first = ci * BANK_COLS + g * ROWS
            for u in range(PAIR):
                for e in range(PAIR):
                    col = PAIR * (BANK_GROUPS * ci + PAIR * g + u) + e
                    nc.scalar.activation(
                        out=a_planes[t][:, PAIR * u + e, first : first + ROWS],
                        in_=halves[:, u, g, :, e],
                        func=ACT.Relu,
                        scale=scales[t][:, col : col + 1],
                        bias=shifts[t][:, col : col + 1],
                    )

        def regroup(t):
            grouped_tile = work.tile([P, BATCH_COLS, PACK], BF16, name="a_grouped", align_bytes=64)
            nc.gpsimd.tensor_scalar(
                out=grouped_tile[:].rearrange("p (c i) t -> p c t i", i=RUN),
                in0=a_planes[t][:].rearrange("p t (c i) -> p c t i", i=RUN),
                scalar1=1.0,
                scalar2=0.0,
                op0=ALU.mult,
                op1=ALU.add,
            )
            a_grouped[t] = grouped_tile

        def transpose_w(t, ci):
            w_ps = ps_w.tile([P, BANK_GROUPS * P], F32)
            transpose_bank(w_ps, w_rows[t], ci)
            w_banks[t, ci] = w_ps

        def copy_w(t, ci):
            if ci == 0:
                grouped_tile = work.tile([P, BATCH_COLS, PACK], BF16, name="w_grouped", align_bytes=64)
                w_grouped[t] = grouped_tile
            part = w_grouped[t][:, ci * BANK_COLS : (ci + 1) * BANK_COLS, :]
            nc.scalar.copy(
                out=part.rearrange("p m t -> p (m t)").bitcast(F32).rearrange("p (m u) -> p m u", u=PAIR),
                in_=w_banks[t, ci][:].rearrange("p (u m) -> p m u", u=PAIR),
            )

        def quantise(grouped, mx, name, t, ci):
            b, r = divmod(t, BLOCK_BATCHES)
            if r == 0 and ci == 0:
                codes_tile = block_pool.tile([P, PASSES * P], U32, name=name + "_codes", align_bytes=64)
                scale_bytes = block_pool.tile([P, PASSES * P], U8, name=name + "_scale_bytes", align_bytes=64)
                mx[b] = (codes_tile, scale_bytes)
            codes_tile, scale_bytes = mx[b]
            first = r * BATCH_COLS + ci * BANK_COLS
            cols = slice(first, first + BANK_COLS)
            nc.vector.quantize_mx(
                out=codes_tile[:, cols].bitcast(FP8X4),
                scales=scale_bytes[:, cols],
                in_=grouped[t][:, ci * BANK_COLS : (ci + 1) * BANK_COLS, :].rearrange("p m t -> p (m t)"),
            )

        def multiply(t):
            b, r = divmod(t, BLOCK_BATCHES)
            a_codes, a_scale_bytes = a_mx[b]
            w_codes, w_scale_bytes = w_mx[b]
            if r == 0:
                acc = ps_acc.tile([P, OUTS], F32)
                accs[b] = acc
            for s in range(r * BATCH_PASSES, (r + 1) * BATCH_PASSES):
                cols = slice(s * P, (s + 1) * P)
                nc.tensor.matmul_mx(
                    out=accs[b][:],
                    lhsT=a_codes[:, cols].bitcast(FP8X4),
                    lhsT_scale=a_scale_bytes[:, cols],
                    rhs=w_codes[:, cols].bitcast(FP8X4),
                    rhs_scale=w_scale_bytes[:, cols],
                    start=(s == 0),
                    stop=(s == PASSES - 1),
                )

        def finish(b):
            result = work.tile([P, OUTS], F32)
            nc.vector.tensor_add(out=result[:], in0=accs[b][:], in1=bias_all[:, b * OUTS : (b + 1) * OUTS])
            nc.sync.dma_start(out=out[b], in_=result[:])

        def live(t):
            return 0 <= t < BATCHES

        with tc.manual_schedule():
            for t in range(PREFETCH):
                load(t)
            nc.sync.dma_start(out=bias_all[:], in_=b7.rearrange("b j -> (b j)").partition_broadcast(P))
            for ci in range(BATCH_BANKS):
                transpose_h(0, ci)
            transpose_w(0, 0)
            for t in range(BATCHES + A_LAG + 1):
                if live(t + PREFETCH):
                    load(t + PREFETCH)
                if live(t - A_LAG - 1):
                    multiply(t - A_LAG - 1)
                if live(t):
                    statistics(t)
                for ci in range(BATCH_BANKS):
                    if live(t + 1):
                        transpose_h(t + 1, ci)
                    for g in range(BANK_PASSES):
                        if live(t - 1):
                            activations(t - 1, ci, g)
                        if live(t) and ci == BATCH_BANKS - 1 and g == 0:
                            spread(t)
                    if live(t):
                        copy_w(t, ci)
                    t_next, ci_next = divmod(t * BATCH_BANKS + ci + 1, BATCH_BANKS)
                    if live(t) and live(t_next):
                        transpose_w(t_next, ci_next)
                if live(t - 1):
                    regroup(t - 1)
                if live(t - A_LAG):
                    quantise(a_grouped, a_mx, "a", t - A_LAG, 0)
                if live(t):
                    gain_times_mean(t)
                if live(t - A_LAG):
                    quantise(a_grouped, a_mx, "a", t - A_LAG, 1)
                if live(t):
                    inverse_spread(t)
                if live(t - 1):
                    quantise(w_grouped, w_mx, "w", t - 1, 0)
                if live(t):
                    scale_terms(t)
                if live(t - 1):
                    quantise(w_grouped, w_mx, "w", t - 1, 1)
                if live(t):
                    shift_term(t)
                if live(t - A_LAG - 1) and (t - A_LAG - 1) % BLOCK_BATCHES == BLOCK_BATCHES - 1:
                    finish((t - A_LAG - 1) // BLOCK_BATCHES)
